import numpy as np
import ml_dtypes


def mxq(x, axis, fmt="e4m3"):
    dtype, down = {"e4m3": (ml_dtypes.float8_e4m3fn, 7), "e5m2": (ml_dtypes.float8_e5m2, 14)}[fmt]
    v = np.moveaxis(np.asarray(x, np.float32).astype(ml_dtypes.bfloat16).astype(np.float64), axis, -1)
    blocks = v.reshape(v.shape[:-1] + (-1, 32))
    amax = np.abs(blocks).max(-1, keepdims=True)
    byte = np.maximum(np.where(amax > 0, np.frexp(amax)[1] - 1 + 127, 0) - down, 1)
    scale = np.exp2(byte - 127.0)
    codes = (blocks / scale).astype(np.float32).astype(dtype).astype(np.float64)
    return np.moveaxis((codes * scale).reshape(v.shape), -1, axis)


BF16 = ml_dtypes.bfloat16


def bf(x):
    return np.asarray(x, np.float32).astype(BF16)


def f64(x):
    return np.asarray(x).astype(np.float64)


B, N, D = 256, 8192, 512

TEMPS = np.array([0.07, 0.1, 0.2])
EPS = 1e-8


def setup_inputs():
    gz = np.exp2(np.random.uniform(-2.0, 2.0, (B, 1)))
    gb = np.exp2(np.random.uniform(-2.0, 2.0, (N, 1)))
    return {"z_ego": bf(np.random.standard_normal((B, D)) * gz),
            "exo_bank": bf(np.random.standard_normal((N, D)) * gb),
            "weights": bf(np.random.standard_normal(len(TEMPS)))}


def reference(z_ego, exo_bank, weights):
    z, e, lw = f64(z_ego), f64(exo_bank), f64(weights)
    zn = z / np.maximum(np.sqrt((z * z).sum(-1, keepdims=True)), EPS)
    bn = e / np.maximum(np.sqrt((e * e).sum(-1, keepdims=True)), EPS)
    sim = mxq(zn, 1, "e4m3") @ mxq(bn, 1, "e4m3").T
    ew = np.exp(lw - lw.max())
    w = ew / ew.sum()
    scale = np.sum(w / TEMPS)
    return sim * scale

@@ -1,0 +1,204 @@
+from contextlib import ExitStack
+
+import concourse.mybir as mybir
+from concourse.masks import make_identity
+
+FLOPS = 2 * 256 * 8192 * 512
+
+F32 = mybir.dt.float32
+BF16 = mybir.dt.bfloat16
+U32 = mybir.dt.uint32
+U8 = mybir.dt.uint8
+FP8X4 = mybir.dt.float8_e4m3fn_x4
+ACT = mybir.ActivationFunctionType
+ALU = mybir.AluOpType
+AX = mybir.AxisListType
+
+P = 128
+D = 512
+HALF = 256
+ROWS = 64
+B = 256
+N = 8192
+Z_TILES = B // ROWS
+N_TILES = N // ROWS
+G_TILES = 8
+GROUPS = N_TILES // G_TILES
+PIECES = [8, 8] + [16] * 7
+TEMPS = (0.07, 0.1, 0.2)
+EPS2 = 1e-16
+STORE_COLS = 1024
+OUT_ON_VECTOR = 22
+
+
+def tile_multiscalecosinefusion_kernel(tc, z_ego, exo_bank, weights, out):
+    nc = tc.nc
+    with ExitStack() as ctx:
+        const = ctx.enter_context(tc.tile_pool(name="const", bufs=1))
+        junkp = ctx.enter_context(tc.tile_pool(name="junkp", bufs=2))
+        small = ctx.enter_context(tc.tile_pool(name="small", bufs=2))
+        xnp = ctx.enter_context(tc.tile_pool(name="xnp", bufs=3))
+        grpp = ctx.enter_context(tc.tile_pool(name="grpp", bufs=3))
+        qp = ctx.enter_context(tc.tile_pool(name="qp", bufs=3))
+        ps_t = ctx.enter_context(tc.psum_pool(name="ps_t", bufs=3))
+        ps_m = ctx.enter_context(tc.psum_pool(name="ps_m", bufs=4))
+        ps_s = ctx.enter_context(tc.psum_pool(name="ps_s", bufs=1))
+
+        wb = const.tile([P, 3], BF16)
+        nc.scalar.dma_start(out=wb[:], in_=weights.partition_broadcast(P))
+        zraw = const.tile([P, Z_TILES, HALF], BF16)
+        z_half = z_ego.rearrange("b (j f) -> (b j) f", j=2)
+        nc.sync.dma_start(out=zraw[:], in_=z_half.rearrange("(t q) f -> q t f", q=P))
+        xraw = const.tile([P, N_TILES, HALF], BF16)
+        e_half = exo_bank.rearrange("n (j f) -> (n j) f", j=2)
+        t0 = 0
+        for cnt in PIECES:
+            nc.sync.dma_start(
+                out=xraw[:, t0 : t0 + cnt, :],
+                in_=e_half[t0 * P : (t0 + cnt) * P, :].rearrange("(t q) f -> q t f", q=P),
+            )
+            t0 += cnt
+
+        ident = const.tile([P, P], BF16)
+        make_identity(nc, ident[:])
+        ident_pairs = ident[:].rearrange("q (w e) -> q w e", e=2)
+        pair_e = const.tile([P, ROWS], F32)
+        nc.vector.tensor_tensor(
+            out=pair_e[:], in0=ident_pairs[:, :, 0], in1=ident_pairs[:, :, 1], op=ALU.add
+        )
+        pair_b = const.tile([P, P], F32)
+        nc.vector.tensor_copy(
+            out=pair_b[:].rearrange("q (w e) -> q w e", e=2),
+            in_=pair_e[:].unsqueeze(2).to_broadcast([P, ROWS, 2]),
+        )
+
+        wf = const.tile([P, 3], F32)
+        nc.vector.tensor_copy(out=wf[:], in_=wb[:])
+        wmax = const.tile([P, 1], F32)
+        nc.vector.reduce_max(out=wmax[:], in_=wf[:], axis=AX.X)
+        nmax = const.tile([P, 1], F32)
+        nc.vector.tensor_scalar(out=nmax[:], in0=wmax[:], scalar1=-1.0, scalar2=None, op0=ALU.mult)
+        ew = const.tile([P, 3], F32)
+        esum = const.tile([P, 1], F32)
+        nc.scalar.activation(
+            out=ew[:], in_=wf[:], func=ACT.Exp, bias=nmax[:, 0:1], scale=1.0, accum_out=esum[:]
+        )
+        num0 = const.tile([P, 1], F32)
+        nc.vector.tensor_scalar(
+            out=num0[:], in0=ew[:, 0:1], scalar1=1.0 / TEMPS[0], scalar2=None, op0=ALU.mult
+        )
+        num1 = const.tile([P, 1], F32)
+        nc.vector.scalar_tensor_tensor(
+            out=num1[:], in0=ew[:, 1:2], scalar=1.0 / TEMPS[1], in1=num0[:], op0=ALU.mult, op1=ALU.add
+        )
+        num2 = const.tile([P, 1], F32)
+        nc.vector.scalar_tensor_tensor(
+            out=num2[:], in0=ew[:, 2:3], scalar=1.0 / TEMPS[2], in1=num1[:], op0=ALU.mult, op1=ALU.add
+        )
+        rsum = const.tile([P, 1], F32)
+        nc.vector.reciprocal(rsum[:], esum[:])
+        scale = const.tile([P, 1], F32)
+        nc.vector.tensor_tensor(out=scale[:], in0=num2[:], in1=rsum[:], op=ALU.mult)
+
+        ssp = const.tile([P, Z_TILES + N_TILES], F32)
+        rinv = const.tile([P, Z_TILES + N_TILES], F32)
+
+        def stats(raw, cnt, col0):
+            for t in range(cnt):
+                junk = junkp.tile([P, HALF], BF16, name="junk")
+                nc.scalar.activation(
+                    out=junk[:],
+                    in_=raw[:, t, :],
+                    func=ACT.Square,
+                    accum_out=ssp[:, col0 + t : col0 + t + 1],
+                )
+            st = ps_s.tile([P, 16], F32, name="st")
+            nc.tensor.matmul(
+                out=st[:, :cnt], lhsT=pair_b[:], rhs=ssp[:, col0 : col0 + cnt], start=True, stop=True
+            )
+            t1 = small.tile([P, 16], F32, name="t1")
+            nc.vector.tensor_scalar(
+                out=t1[:, :cnt], in0=st[:, :cnt], scalar1=EPS2, scalar2=None, op0=ALU.max
+            )
+            t2 = small.tile([P, 16], F32, name="t2")
+            nc.vector.reciprocal(t2[:, :cnt], t1[:, :cnt])
+            nc.scalar.activation(out=rinv[:, col0 : col0 + cnt], in_=t2[:, :cnt], func=ACT.Sqrt)
+
+        def to_columns(raw, cnt, col0, grp):
+            xn = xnp.tile([P, G_TILES, HALF], BF16, name="xn")
+            for t in range(cnt):
+                nc.vector.tensor_scalar(
+                    out=xn[:, t, :],
+                    in0=raw[:, t, :],
+                    scalar1=rinv[:, col0 + t : col0 + t + 1],
+                    scalar2=None,
+                    op0=ALU.mult,
+                )
+            for h in range(cnt // 4):
+                pt = ps_t.tile([P, 4 * ROWS, 4], BF16, name="pt")
+                for tb in range(4):
+                    for u in range(2):
+                        nc.tensor.transpose(
+                            pt[:, ROWS * tb : ROWS * (tb + 1), 2 * u : 2 * u + 2],
+                            xn[:, 4 * h + tb, P * u : P * (u + 1)],
+                            ident[:],
+                        )
+                nc.vector.tensor_copy(
+                    out=grp[:, 1024 * h : 1024 * (h + 1)], in_=pt[:].rearrange("p c t -> p (c t)")
+                )
+
+        stats(zraw, Z_TILES, 0)
+        zgrp = const.tile([P, 4 * B], BF16, align_bytes=64)
+        to_columns(zraw, Z_TILES, 0, zgrp)
+        zc = const.tile([P, B], U32, align_bytes=64)
+        zs = const.tile([P, B], U8, align_bytes=64)
+        nc.vector.quantize_mx(out=zc[:].bitcast(FP8X4), scales=zs[:], in_=zgrp[:])
+
+        stage = [const.tile([P, N], F32, name="stage%d" % m) for m in range(2)]
+        piece_start = []
+        t0 = 0
+        for cnt in PIECES:
+            piece_start.append(t0)
+            t0 += cnt
+        done = [0]
+
+        def stats_up_to(tile_end):
+            while done[0] < len(PIECES) and piece_start[done[0]] < tile_end:
+                k = done[0]
+                stats(xraw[:, piece_start[k] : piece_start[k] + PIECES[k], :], PIECES[k], Z_TILES + piece_start[k])
+                done[0] += 1
+
+        bank_no = 0
+        for g in range(GROUPS):
+            stats_up_to(min(N_TILES, (g + 3) * G_TILES))
+            grp = grpp.tile([P, 4 * D], BF16, name="grp", align_bytes=64)
+            to_columns(xraw[:, g * G_TILES : (g + 1) * G_TILES, :], G_TILES, Z_TILES + g * G_TILES, grp)
+            codes = qp.tile([P, D], U32, name="codes", align_bytes=64)
+            scl = qp.tile([P, D], U8, name="scl", align_bytes=64)
+            nc.vector.quantize_mx(out=codes[:].bitcast(FP8X4), scales=scl[:], in_=grp[:])
+            for m in range(2):
+                acc = ps_m.tile([P, D], F32, name="acc")
+                nc.tensor.matmul_mx(
+                    out=acc[:],
+                    lhsT=zc[:, m * P : (m + 1) * P].bitcast(FP8X4),
+                    lhsT_scale=zs[:, m * P : (m + 1) * P],
+                    rhs=codes[:].bitcast(FP8X4),
+                    rhs_scale=scl[:],
+                    start=True,
+                    stop=True,
+                )
+                dst = stage[m][:, g * D : (g + 1) * D]
+                if (bank_no * OUT_ON_VECTOR) % 32 < OUT_ON_VECTOR:
+                    nc.vector.tensor_scalar(
+                        out=dst, in0=acc[:], scalar1=scale[:, 0:1], scalar2=None, op0=ALU.mult
+                    )
+                else:
+                    nc.scalar.activation(out=dst, in_=acc[:], func=ACT.Copy, scale=scale[:, 0:1])
+                bank_no += 1
+            if (g + 1) * D % STORE_COLS == 0:
+                c1 = (g + 1) * D
+                for m in range(2):
+                    nc.sync.dma_start(
+                        out=out[m * P : (m + 1) * P, c1 - STORE_COLS : c1],
+                        in_=stage[m][:, c1 - STORE_COLS : c1],
+                    )

@@ -16,19 +16,15 @@ AX = mybir.AxisListType
 
 P = 128
 D = 512
-HALF = 256
-ROWS = 64
 B = 256
 N = 8192
-Z_TILES = B // ROWS
-N_TILES = N // ROWS
-G_TILES = 8
-GROUPS = N_TILES // G_TILES
-PIECES = [8, 8] + [16] * 7
-TEMPS = (0.07, 0.1, 0.2)
-EPS2 = 1e-16
-STORE_COLS = 1024
-OUT_ON_VECTOR = 22
+ZJ = B // P
+GJ = 4
+GROUP = GJ * P
+GROUPS = N // GROUP
+INV_TEMPS = (1.0 / 0.07, 1.0 / 0.1, 1.0 / 0.2)
+LOG2E = 1.4426950408889634
+MAX_RINV = 1e8
 
 
 def tile_multiscalecosinefusion_kernel(tc, z_ego, exo_bank, weights, out):
@@ -36,169 +32,223 @@ def tile_multiscalecosinefusion_kernel(tc, z_ego, exo_bank, weights, out):
     with ExitStack() as ctx:
         const = ctx.enter_context(tc.tile_pool(name="const", bufs=1))
         junkp = ctx.enter_context(tc.tile_pool(name="junkp", bufs=2))
-        small = ctx.enter_context(tc.tile_pool(name="small", bufs=2))
         xnp = ctx.enter_context(tc.tile_pool(name="xnp", bufs=3))
         grpp = ctx.enter_context(tc.tile_pool(name="grpp", bufs=3))
         qp = ctx.enter_context(tc.tile_pool(name="qp", bufs=3))
-        ps_t = ctx.enter_context(tc.psum_pool(name="ps_t", bufs=3))
+        ps_t = ctx.enter_context(tc.psum_pool(name="ps_t", bufs=4))
         ps_m = ctx.enter_context(tc.psum_pool(name="ps_m", bufs=4))
-        ps_s = ctx.enter_context(tc.psum_pool(name="ps_s", bufs=1))
+        ctx.enter_context(tc.manual_schedule())
 
-        wb = const.tile([P, 3], BF16)
-        nc.scalar.dma_start(out=wb[:], in_=weights.partition_broadcast(P))
-        zraw = const.tile([P, Z_TILES, HALF], BF16)
-        z_half = z_ego.rearrange("b (j f) -> (b j) f", j=2)
-        nc.sync.dma_start(out=zraw[:], in_=z_half.rearrange("(t q) f -> q t f", q=P))
-        xraw = const.tile([P, N_TILES, HALF], BF16)
-        e_half = exo_bank.rearrange("n (j f) -> (n j) f", j=2)
-        t0 = 0
-        for cnt in PIECES:
-            nc.sync.dma_start(
-                out=xraw[:, t0 : t0 + cnt, :],
-                in_=e_half[t0 * P : (t0 + cnt) * P, :].rearrange("(t q) f -> q t f", q=P),
-            )
-            t0 += cnt
+        zraw = const.tile([P, ZJ, D], BF16)
+        xraw = const.tile([P, GROUPS, GJ, D], BF16)
+        wrow = const.tile([P, 4], BF16)
+        bank = exo_bank.rearrange("(g p j) d -> p g j d", p=P, j=GJ)
+        nc.vector.memset(wrow[:], 0.0)
+        nc.sync.dma_start(out=zraw[:], in_=z_ego.rearrange("(p j) d -> p j d", j=ZJ))
+        nc.sync.dma_start(out=xraw[:, 0, 0:2, :], in_=bank[:, 0, 0:2, :])
+        nc.sync.dma_start(out=xraw[:, 0, 2:4, :], in_=bank[:, 0, 2:4, :])
+        nc.sync.dma_start(out=wrow[0:1, 0:3], in_=weights.unsqueeze(0))
+        for g in range(1, 4):
+            nc.sync.dma_start(out=xraw[:, g, :, :], in_=bank[:, g, :, :])
+        for g in range(4, GROUPS, 2):
+            nc.sync.dma_start(out=xraw[:, g : g + 2, :, :], in_=bank[:, g : g + 2, :, :])
 
-        ident = const.tile([P, P], BF16)
+        ones = const.tile([P, P], BF16)
+        nc.vector.memset(ones[:], 1.0)
+        two = const.tile([P, 3], F32)
+        nc.vector.memset(two[:], 2.0)
+        minus1 = const.tile([P, 1], F32)
+        nc.vector.memset(minus1[:], -1.0)
+        warm = const.tile([P, 1], F32)
+        nc.scalar.activation(out=warm[:], in_=minus1[:], func=ACT.Abs_reciprocal_sqrt)
+        ident = const.tile([P, P], F32)
         make_identity(nc, ident[:])
-        ident_pairs = ident[:].rearrange("q (w e) -> q w e", e=2)
-        pair_e = const.tile([P, ROWS], F32)
-        nc.vector.tensor_tensor(
-            out=pair_e[:], in0=ident_pairs[:, :, 0], in1=ident_pairs[:, :, 1], op=ALU.add
-        )
-        pair_b = const.tile([P, P], F32)
-        nc.vector.tensor_copy(
-            out=pair_b[:].rearrange("q (w e) -> q w e", e=2),
-            in_=pair_e[:].unsqueeze(2).to_broadcast([P, ROWS, 2]),
-        )
 
-        wf = const.tile([P, 3], F32)
-        nc.vector.tensor_copy(out=wf[:], in_=wb[:])
-        wmax = const.tile([P, 1], F32)
-        nc.vector.reduce_max(out=wmax[:], in_=wf[:], axis=AX.X)
-        nmax = const.tile([P, 1], F32)
-        nc.vector.tensor_scalar(out=nmax[:], in0=wmax[:], scalar1=-1.0, scalar2=None, op0=ALU.mult)
-        ew = const.tile([P, 3], F32)
-        esum = const.tile([P, 1], F32)
-        nc.scalar.activation(
-            out=ew[:], in_=wf[:], func=ACT.Exp, bias=nmax[:, 0:1], scale=1.0, accum_out=esum[:]
-        )
-        num0 = const.tile([P, 1], F32)
-        nc.vector.tensor_scalar(
-            out=num0[:], in0=ew[:, 0:1], scalar1=1.0 / TEMPS[0], scalar2=None, op0=ALU.mult
-        )
-        num1 = const.tile([P, 1], F32)
-        nc.vector.scalar_tensor_tensor(
-            out=num1[:], in0=ew[:, 1:2], scalar=1.0 / TEMPS[1], in1=num0[:], op0=ALU.mult, op1=ALU.add
-        )
-        num2 = const.tile([P, 1], F32)
-        nc.vector.scalar_tensor_tensor(
-            out=num2[:], in0=ew[:, 2:3], scalar=1.0 / TEMPS[2], in1=num1[:], op0=ALU.mult, op1=ALU.add
-        )
-        rsum = const.tile([P, 1], F32)
-        nc.vector.reciprocal(rsum[:], esum[:])
-        scale = const.tile([P, 1], F32)
-        nc.vector.tensor_tensor(out=scale[:], in0=num2[:], in1=rsum[:], op=ALU.mult)
+        ssp = const.tile([P, ZJ + GROUPS * GJ], F32)
+        rsq = const.tile([P, ZJ + GROUPS * GJ], F32)
+        rinv = const.tile([P, ZJ + GROUPS * GJ], F32)
+        stage = const.tile([P, GROUPS, 2, GROUP], F32)
 
-        ssp = const.tile([P, Z_TILES + N_TILES], F32)
-        rinv = const.tile([P, Z_TILES + N_TILES], F32)
+        def col(g):
+            return 0 if g < 0 else ZJ + g * GJ
 
-        def stats(raw, cnt, col0):
-            for t in range(cnt):
-                junk = junkp.tile([P, HALF], BF16, name="junk")
-                nc.scalar.activation(
-                    out=junk[:],
-                    in_=raw[:, t, :],
-                    func=ACT.Square,
-                    accum_out=ssp[:, col0 + t : col0 + t + 1],
-                )
-            st = ps_s.tile([P, 16], F32, name="st")
-            nc.tensor.matmul(
-                out=st[:, :cnt], lhsT=pair_b[:], rhs=ssp[:, col0 : col0 + cnt], start=True, stop=True
+        def rows(g):
+            return ZJ if g < 0 else GJ
+
+        def raw(g, j):
+            return zraw[:, j, :] if g < 0 else xraw[:, g, j, :]
+
+        def square_s(g, j):
+            junk = junkp.tile([P, D], BF16, name="junk_s")
+            c = col(g) + j
+            nc.scalar.activation(out=junk[:], in_=raw(g, j), func=ACT.Square, accum_out=ssp[:, c : c + 1])
+
+        def square_v(g, j):
+            junk = junkp.tile([P, D], BF16, name="junk_v")
+            c = col(g) + j
+            nc.vector.scalar_tensor_tensor(
+                out=junk[:], in0=raw(g, j), scalar=1.0, in1=raw(g, j), op0=ALU.mult, op1=ALU.mult,
+                accum_out=ssp[:, c : c + 1],
             )
-            t1 = small.tile([P, 16], F32, name="t1")
-            nc.vector.tensor_scalar(
-                out=t1[:, :cnt], in0=st[:, :cnt], scalar1=EPS2, scalar2=None, op0=ALU.max
-            )
-            t2 = small.tile([P, 16], F32, name="t2")
-            nc.vector.reciprocal(t2[:, :cnt], t1[:, :cnt])
-            nc.scalar.activation(out=rinv[:, col0 : col0 + cnt], in_=t2[:, :cnt], func=ACT.Sqrt)
 
-        def to_columns(raw, cnt, col0, grp):
-            xn = xnp.tile([P, G_TILES, HALF], BF16, name="xn")
-            for t in range(cnt):
+        def root(g):
+            c = slice(col(g), col(g) + rows(g))
+            nc.scalar.activation(out=rsq[:, c], in_=ssp[:, c], func=ACT.Abs_reciprocal_sqrt)
+
+        def clamp(g):
+            c = slice(col(g), col(g) + rows(g))
+            nc.vector.tensor_scalar(out=rinv[:, c], in0=rsq[:, c], scalar1=MAX_RINV, scalar2=None, op0=ALU.min)
+
+        xn = {}
+        pt = {}
+        grp = {}
+        codes = {}
+        acc = {}
+
+        def normalise(g):
+            t = xnp.tile([P, GJ, D], BF16, name="xn")
+            xn[g] = t
+            for j in range(rows(g)):
+                c = col(g) + j
                 nc.vector.tensor_scalar(
-                    out=xn[:, t, :],
-                    in0=raw[:, t, :],
-                    scalar1=rinv[:, col0 + t : col0 + t + 1],
-                    scalar2=None,
-                    op0=ALU.mult,
+                    out=t[:, j, :], in0=raw(g, j), scalar1=rinv[:, c : c + 1], scalar2=None, op0=ALU.mult
                 )
-            for h in range(cnt // 4):
-                pt = ps_t.tile([P, 4 * ROWS, 4], BF16, name="pt")
-                for tb in range(4):
+
+        def transposes(g):
+            for h in range(rows(g) // 2):
+                t = ps_t.tile([P, 2, 2, P], F32, name="pt")
+                pt[g, h] = t
+                for j in range(2):
+                    words = xn[g][:, 2 * h + j, :].bitcast(F32)
                     for u in range(2):
-                        nc.tensor.transpose(
-                            pt[:, ROWS * tb : ROWS * (tb + 1), 2 * u : 2 * u + 2],
-                            xn[:, 4 * h + tb, P * u : P * (u + 1)],
-                            ident[:],
-                        )
-                nc.vector.tensor_copy(
-                    out=grp[:, 1024 * h : 1024 * (h + 1)], in_=pt[:].rearrange("p c t -> p (c t)")
-                )
+                        nc.tensor.transpose(t[:, j, u, :], words[:, u * P : (u + 1) * P], ident[:])
 
-        stats(zraw, Z_TILES, 0)
-        zgrp = const.tile([P, 4 * B], BF16, align_bytes=64)
-        to_columns(zraw, Z_TILES, 0, zgrp)
-        zc = const.tile([P, B], U32, align_bytes=64)
-        zs = const.tile([P, B], U8, align_bytes=64)
-        nc.vector.quantize_mx(out=zc[:].bitcast(FP8X4), scales=zs[:], in_=zgrp[:])
+        def new_grp(g):
+            t = grpp.tile([P, GROUP * 4], BF16, name="grp", align_bytes=64)
+            grp[g] = t
 
-        stage = [const.tile([P, N], F32, name="stage%d" % m) for m in range(2)]
-        piece_start = []
-        t0 = 0
-        for cnt in PIECES:
-            piece_start.append(t0)
-            t0 += cnt
-        done = [0]
+        def copy_out(g, h, engine):
+            dst = grp[g][:, h * 1024 : (h + 1) * 1024].bitcast(F32).rearrange("p (j r u) -> p j r u", j=2, u=2)
+            src = pt[g, h][:].rearrange("p j u r -> p j r u")
+            if engine == "v":
+                nc.vector.tensor_copy(out=dst, in_=src)
+            else:
+                nc.scalar.copy(out=dst, in_=src)
 
-        def stats_up_to(tile_end):
-            while done[0] < len(PIECES) and piece_start[done[0]] < tile_end:
-                k = done[0]
-                stats(xraw[:, piece_start[k] : piece_start[k] + PIECES[k], :], PIECES[k], Z_TILES + piece_start[k])
-                done[0] += 1
+        def quantise(g):
+            w = rows(g) * P
+            c = qp.tile([P, GROUP], U32, name="codes", align_bytes=64)
+            s = qp.tile([P, GROUP], U8, name="scl", align_bytes=64)
+            codes[g] = (c, s)
+            nc.vector.quantize_mx(out=c[:, :w].bitcast(FP8X4), scales=s[:, :w], in_=grp[g][:, : 4 * w])
 
-        bank_no = 0
-        for g in range(GROUPS):
-            stats_up_to(min(N_TILES, (g + 3) * G_TILES))
-            grp = grpp.tile([P, 4 * D], BF16, name="grp", align_bytes=64)
-            to_columns(xraw[:, g * G_TILES : (g + 1) * G_TILES, :], G_TILES, Z_TILES + g * G_TILES, grp)
-            codes = qp.tile([P, D], U32, name="codes", align_bytes=64)
-            scl = qp.tile([P, D], U8, name="scl", align_bytes=64)
-            nc.vector.quantize_mx(out=codes[:].bitcast(FP8X4), scales=scl[:], in_=grp[:])
+        def multiply(g):
             for m in range(2):
-                acc = ps_m.tile([P, D], F32, name="acc")
+                a = ps_m.tile([P, GROUP], F32, name="acc")
+                acc[g, m] = a
                 nc.tensor.matmul_mx(
-                    out=acc[:],
+                    out=a[:],
                     lhsT=zc[:, m * P : (m + 1) * P].bitcast(FP8X4),
                     lhsT_scale=zs[:, m * P : (m + 1) * P],
-                    rhs=codes[:].bitcast(FP8X4),
-                    rhs_scale=scl[:],
+                    rhs=codes[g][0][:].bitcast(FP8X4),
+                    rhs_scale=codes[g][1][:],
                     start=True,
                     stop=True,
                 )
-                dst = stage[m][:, g * D : (g + 1) * D]
-                if (bank_no * OUT_ON_VECTOR) % 32 < OUT_ON_VECTOR:
-                    nc.vector.tensor_scalar(
-                        out=dst, in0=acc[:], scalar1=scale[:, 0:1], scalar2=None, op0=ALU.mult
-                    )
-                else:
-                    nc.scalar.activation(out=dst, in_=acc[:], func=ACT.Copy, scale=scale[:, 0:1])
-                bank_no += 1
-            if (g + 1) * D % STORE_COLS == 0:
-                c1 = (g + 1) * D
-                for m in range(2):
-                    nc.sync.dma_start(
-                        out=out[m * P : (m + 1) * P, c1 - STORE_COLS : c1],
-                        in_=stage[m][:, c1 - STORE_COLS : c1],
-                    )
+
+        def result(g, m, engine):
+            dst = stage[:, g, m, :].rearrange("p (r j) -> p r j", j=GJ)
+            src = acc[g, m][:].rearrange("p (j r) -> p r j", j=GJ)
+            if engine == "v":
+                nc.vector.tensor_scalar(out=dst, in0=src, scalar1=scale[:, 0:1], scalar2=None, op0=ALU.mult)
+            else:
+                nc.scalar.activation(out=dst, in_=src, func=ACT.Copy, scale=scale[:, 0:1])
+
+        out_rows = out.rearrange("(p m) n -> p m n", m=2)
+
+        def store(g0, g1):
+            for g in range(g0, g1):
+                nc.sync.dma_start(out=out_rows[:, :, g * GROUP : (g + 1) * GROUP], in_=stage[:, g, :, :])
+
+        square_s(-1, 0)
+        square_v(-1, 1)
+        square_s(0, 0)
+        square_v(0, 2)
+        root(-1)
+        square_s(0, 1)
+        square_v(0, 3)
+        clamp(-1)
+
+        wps = ps_m.tile([P, GROUP], F32, name="acc")
+        nc.tensor.matmul(out=wps[:, 0:4], lhsT=ones[:], rhs=wrow[:], start=True, stop=True)
+        wf = const.tile([P, 3], F32)
+        nc.vector.tensor_copy(out=wf[:], in_=wps[:, 0:3])
+        wmax = const.tile([P, 1], F32)
+        nc.vector.reduce_max(out=wmax[:], in_=wps[:, 0:3], axis=AX.X)
+
+        wd = const.tile([P, 3], F32)
+        nc.gpsimd.tensor_scalar(
+            out=wd[:], in0=wf[:], scalar1=wmax[:, 0:1], scalar2=None, op0=ALU.subtract
+        )
+        wl = const.tile([P, 3], F32)
+        nc.gpsimd.tensor_scalar(out=wl[:], in0=wd[:], scalar1=LOG2E, scalar2=None, op0=ALU.mult)
+        ew = const.tile([P, 3], F32)
+        nc.gpsimd.tensor_tensor(out=ew[:], in0=two[:], in1=wl[:], op=ALU.pow)
+        terms = const.tile([P, 3], F32)
+        for i in range(3):
+            nc.gpsimd.tensor_scalar(
+                out=terms[:, i : i + 1], in0=ew[:, i : i + 1], scalar1=INV_TEMPS[i], scalar2=None, op0=ALU.mult
+            )
+        s01 = const.tile([P, 1], F32)
+        nc.gpsimd.tensor_tensor(out=s01[:], in0=ew[:, 0:1], in1=ew[:, 1:2], op=ALU.add)
+        s012 = const.tile([P, 1], F32)
+        nc.gpsimd.tensor_tensor(out=s012[:], in0=s01[:], in1=ew[:, 2:3], op=ALU.add)
+        n01 = const.tile([P, 1], F32)
+        nc.gpsimd.tensor_tensor(out=n01[:], in0=terms[:, 0:1], in1=terms[:, 1:2], op=ALU.add)
+        n012 = const.tile([P, 1], F32)
+        nc.gpsimd.tensor_tensor(out=n012[:], in0=n01[:], in1=terms[:, 2:3], op=ALU.add)
+        rsum = const.tile([P, 1], F32)
+        nc.gpsimd.tensor_tensor(out=rsum[:], in0=s012[:], in1=minus1[:], op=ALU.pow)
+        scale = const.tile([P, 1], F32)
+        nc.gpsimd.tensor_tensor(out=scale[:], in0=n012[:], in1=rsum[:], op=ALU.mult)
+
+        normalise(-1)
+        root(0)
+        clamp(0)
+        transposes(-1)
+        new_grp(-1)
+        copy_out(-1, 0, "v")
+        normalise(0)
+        transposes(0)
+        for j in range(GJ):
+            square_s(1, j)
+        zc = const.tile([P, B], U32, align_bytes=64)
+        zs = const.tile([P, B], U8, align_bytes=64)
+        nc.vector.quantize_mx(out=zc[:].bitcast(FP8X4), scales=zs[:], in_=grp[-1][:, : 4 * B])
+
+        for g in range(GROUPS + 1):
+            if g == 0:
+                root(1)
+            late = g >= GROUPS - 2
+            if g + 2 < GROUPS:
+                for j in range(GJ):
+                    square_s(g + 2, j)
+            if g < GROUPS:
+                new_grp(g)
+                copy_out(g, 0, "v")
+            if g + 1 < GROUPS:
+                clamp(g + 1)
+            if g < GROUPS:
+                copy_out(g, 1, "s" if late else "v")
+            if g + 1 < GROUPS:
+                normalise(g + 1)
+                transposes(g + 1)
+            if g < GROUPS:
+                quantise(g)
+                multiply(g)
+            if g > 0:
+                result(g - 1, 0, "s" if late and g < GROUPS else "v")
+                result(g - 1, 1, "s")
+                store(g - 1, g)
+            if g + 2 < GROUPS:
+                root(g + 2)

@@ -18,10 +18,14 @@ P = 128
 D = 512
 B = 256
 N = 8192
+TILES = N // P
 ZJ = B // P
-GJ = 4
-GROUP = GJ * P
-GROUPS = N // GROUP
+SIZES = [4] * 15 + [2, 2]
+STARTS = [sum(SIZES[:u]) for u in range(len(SIZES))]
+UNITS = len(SIZES)
+MAXJ = max(SIZES)
+LAST = UNITS - 2
+Z = -1
 INV_TEMPS = (1.0 / 0.07, 1.0 / 0.1, 1.0 / 0.2)
 LOG2E = 1.4426950408889634
 MAX_RINV = 1e8
@@ -32,7 +36,7 @@ def tile_multiscalecosinefusion_kernel(tc, z_ego, exo_bank, weights, out):
     with ExitStack() as ctx:
         const = ctx.enter_context(tc.tile_pool(name="const", bufs=1))
         junkp = ctx.enter_context(tc.tile_pool(name="junkp", bufs=2))
-        xnp = ctx.enter_context(tc.tile_pool(name="xnp", bufs=3))
+        xnp = ctx.enter_context(tc.tile_pool(name="xnp", bufs=4))
         grpp = ctx.enter_context(tc.tile_pool(name="grpp", bufs=3))
         qp = ctx.enter_context(tc.tile_pool(name="qp", bufs=3))
         ps_t = ctx.enter_context(tc.psum_pool(name="ps_t", bufs=4))
@@ -40,18 +44,26 @@ def tile_multiscalecosinefusion_kernel(tc, z_ego, exo_bank, weights, out):
         ctx.enter_context(tc.manual_schedule())
 
         zraw = const.tile([P, ZJ, D], BF16)
-        xraw = const.tile([P, GROUPS, GJ, D], BF16)
+        xraw = const.tile([P, TILES, D], BF16)
         wrow = const.tile([P, 4], BF16)
-        bank = exo_bank.rearrange("(g p j) d -> p g j d", p=P, j=GJ)
         nc.vector.memset(wrow[:], 0.0)
-        nc.sync.dma_start(out=zraw[:], in_=z_ego.rearrange("(p j) d -> p j d", j=ZJ))
-        nc.sync.dma_start(out=xraw[:, 0, 0:2, :], in_=bank[:, 0, 0:2, :])
-        nc.sync.dma_start(out=xraw[:, 0, 2:4, :], in_=bank[:, 0, 2:4, :])
-        nc.sync.dma_start(out=wrow[0:1, 0:3], in_=weights.unsqueeze(0))
-        for g in range(1, 4):
-            nc.sync.dma_start(out=xraw[:, g, :, :], in_=bank[:, g, :, :])
-        for g in range(4, GROUPS, 2):
-            nc.sync.dma_start(out=xraw[:, g : g + 2, :, :], in_=bank[:, g : g + 2, :, :])
+
+        def rows_of(u):
+            return exo_bank[STARTS[u] * P : (STARTS[u] + SIZES[u]) * P, :].rearrange("(p j) d -> p j d", p=P)
+
+        def load(u, j0, j1):
+            nc.sync.dma_start(out=xraw[:, STARTS[u] + j0 : STARTS[u] + j1, :], in_=rows_of(u)[:, j0:j1, :])
+
+        z_rows = z_ego.rearrange("(p j) d -> p j d", j=ZJ)
+        for j in range(ZJ):
+            nc.sync.dma_start(out=zraw[:, j, :], in_=z_rows[:, j, :])
+        for u in range(3):
+            load(u, 0, 2)
+            load(u, 2, 4)
+            if u == 0:
+                nc.sync.dma_start(out=wrow[0:1, 0:3], in_=weights.unsqueeze(0))
+        for u in range(3, UNITS):
+            load(u, 0, SIZES[u])
 
         ones = const.tile([P, P], BF16)
         nc.vector.memset(ones[:], 1.0)
@@ -64,39 +76,39 @@ def tile_multiscalecosinefusion_kernel(tc, z_ego, exo_bank, weights, out):
         ident = const.tile([P, P], F32)
         make_identity(nc, ident[:])
 
-        ssp = const.tile([P, ZJ + GROUPS * GJ], F32)
-        rsq = const.tile([P, ZJ + GROUPS * GJ], F32)
-        rinv = const.tile([P, ZJ + GROUPS * GJ], F32)
-        stage = const.tile([P, GROUPS, 2, GROUP], F32)
+        ssp = const.tile([P, ZJ + TILES], F32)
+        rsq = const.tile([P, ZJ + TILES], F32)
+        rinv = const.tile([P, ZJ + TILES], F32)
+        stage = const.tile([P, 2 * N], F32)
 
-        def col(g):
-            return 0 if g < 0 else ZJ + g * GJ
+        def size(u):
+            return ZJ if u == Z else SIZES[u]
 
-        def rows(g):
-            return ZJ if g < 0 else GJ
+        def col(u):
+            return 0 if u == Z else ZJ + STARTS[u]
 
-        def raw(g, j):
-            return zraw[:, j, :] if g < 0 else xraw[:, g, j, :]
+        def raw(u, j):
+            return zraw[:, j, :] if u == Z else xraw[:, STARTS[u] + j, :]
 
-        def square_s(g, j):
+        def square_s(u, j):
             junk = junkp.tile([P, D], BF16, name="junk_s")
-            c = col(g) + j
-            nc.scalar.activation(out=junk[:], in_=raw(g, j), func=ACT.Square, accum_out=ssp[:, c : c + 1])
+            c = col(u) + j
+            nc.scalar.activation(out=junk[:], in_=raw(u, j), func=ACT.Square, accum_out=ssp[:, c : c + 1])
 
-        def square_v(g, j):
+        def square_v(u, j):
             junk = junkp.tile([P, D], BF16, name="junk_v")
-            c = col(g) + j
+            c = col(u) + j
             nc.vector.scalar_tensor_tensor(
-                out=junk[:], in0=raw(g, j), scalar=1.0, in1=raw(g, j), op0=ALU.mult, op1=ALU.mult,
+                out=junk[:], in0=raw(u, j), scalar=1.0, in1=raw(u, j), op0=ALU.mult, op1=ALU.mult,
                 accum_out=ssp[:, c : c + 1],
             )
 
-        def root(g):
-            c = slice(col(g), col(g) + rows(g))
+        def root(u):
+            c = slice(col(u), col(u) + size(u))
             nc.scalar.activation(out=rsq[:, c], in_=ssp[:, c], func=ACT.Abs_reciprocal_sqrt)
 
-        def clamp(g):
-            c = slice(col(g), col(g) + rows(g))
+        def clamp(u):
+            c = slice(col(u), col(u) + size(u))
             nc.vector.tensor_scalar(out=rinv[:, c], in0=rsq[:, c], scalar1=MAX_RINV, scalar2=None, op0=ALU.min)
 
         xn = {}
@@ -105,60 +117,67 @@ def tile_multiscalecosinefusion_kernel(tc, z_ego, exo_bank, weights, out):
         codes = {}
         acc = {}
 
-        def normalise(g):
-            t = xnp.tile([P, GJ, D], BF16, name="xn")
-            xn[g] = t
-            for j in range(rows(g)):
-                c = col(g) + j
+        def normalise(u):
+            t = xnp.tile([P, MAXJ, D], BF16, name="xn")
+            xn[u] = t
+            for j in range(size(u)):
+                c = col(u) + j
                 nc.vector.tensor_scalar(
-                    out=t[:, j, :], in0=raw(g, j), scalar1=rinv[:, c : c + 1], scalar2=None, op0=ALU.mult
+                    out=t[:, j, :], in0=raw(u, j), scalar1=rinv[:, c : c + 1], scalar2=None, op0=ALU.mult
                 )
 
-        def transposes(g):
-            for h in range(rows(g) // 2):
+        def transposes(u):
+            for h in range(size(u) // 2):
                 t = ps_t.tile([P, 2, 2, P], F32, name="pt")
-                pt[g, h] = t
+                pt[u, h] = t
                 for j in range(2):
-                    words = xn[g][:, 2 * h + j, :].bitcast(F32)
-                    for u in range(2):
-                        nc.tensor.transpose(t[:, j, u, :], words[:, u * P : (u + 1) * P], ident[:])
+                    words = xn[u][:, 2 * h + j, :].bitcast(F32)
+                    for w in range(2):
+                        nc.tensor.transpose(t[:, j, w, :], words[:, w * P : (w + 1) * P], ident[:])
 
-        def new_grp(g):
-            t = grpp.tile([P, GROUP * 4], BF16, name="grp", align_bytes=64)
-            grp[g] = t
+        def new_grp(u):
+            t = grpp.tile([P, MAXJ * P * 4], BF16, name="grp", align_bytes=64)
+            grp[u] = t
 
-        def copy_out(g, h, engine):
-            dst = grp[g][:, h * 1024 : (h + 1) * 1024].bitcast(F32).rearrange("p (j r u) -> p j r u", j=2, u=2)
-            src = pt[g, h][:].rearrange("p j u r -> p j r u")
+        def copy_out(u, h, engine):
+            dst = grp[u][:, h * 1024 : (h + 1) * 1024].bitcast(F32).rearrange("p (j r w) -> p j r w", j=2, w=2)
+            src = pt[u, h][:].rearrange("p j w r -> p j r w")
             if engine == "v":
                 nc.vector.tensor_copy(out=dst, in_=src)
             else:
                 nc.scalar.copy(out=dst, in_=src)
 
-        def quantise(g):
-            w = rows(g) * P
-            c = qp.tile([P, GROUP], U32, name="codes", align_bytes=64)
-            s = qp.tile([P, GROUP], U8, name="scl", align_bytes=64)
-            codes[g] = (c, s)
-            nc.vector.quantize_mx(out=c[:, :w].bitcast(FP8X4), scales=s[:, :w], in_=grp[g][:, : 4 * w])
+        def quantise(u):
+            n = size(u) * P
+            c = qp.tile([P, MAXJ * P], U32, name="codes", align_bytes=64)
+            s = qp.tile([P, MAXJ * P], U8, name="scl", align_bytes=64)
+            codes[u] = (c, s)
+            nc.vector.quantize_mx(out=c[:, :n].bitcast(FP8X4), scales=s[:, :n], in_=grp[u][:, : 4 * n])
 
-        def multiply(g):
+        def multiply(u):
+            n = size(u) * P
             for m in range(2):
-                a = ps_m.tile([P, GROUP], F32, name="acc")
-                acc[g, m] = a
+                if size(u) < MAXJ:
+                    a = ps_t.tile([P, 2, 2, P], F32, name="pt")
+                    a = a[:].rearrange("p j w r -> p (j w r)")
+                else:
+                    a = ps_m.tile([P, MAXJ * P], F32, name="acc")
+                acc[u, m] = a
                 nc.tensor.matmul_mx(
-                    out=a[:],
+                    out=a[:, :n],
                     lhsT=zc[:, m * P : (m + 1) * P].bitcast(FP8X4),
                     lhsT_scale=zs[:, m * P : (m + 1) * P],
-                    rhs=codes[g][0][:].bitcast(FP8X4),
-                    rhs_scale=codes[g][1][:],
+                    rhs=codes[u][0][:, :n].bitcast(FP8X4),
+                    rhs_scale=codes[u][1][:, :n],
                     start=True,
                     stop=True,
                 )
 
-        def result(g, m, engine):
-            dst = stage[:, g, m, :].rearrange("p (r j) -> p r j", j=GJ)
-            src = acc[g, m][:].rearrange("p (j r) -> p r j", j=GJ)
+        def result(u, m, engine):
+            n = size(u) * P
+            n0 = 2 * STARTS[u] * P + m * n
+            dst = stage[:, n0 : n0 + n].rearrange("p (r j) -> p r j", j=size(u))
+            src = acc[u, m][:, :n].rearrange("p (j r) -> p r j", j=size(u))
             if engine == "v":
                 nc.vector.tensor_scalar(out=dst, in0=src, scalar1=scale[:, 0:1], scalar2=None, op0=ALU.mult)
             else:
@@ -166,21 +185,43 @@ def tile_multiscalecosinefusion_kernel(tc, z_ego, exo_bank, weights, out):
 
         out_rows = out.rearrange("(p m) n -> p m n", m=2)
 
-        def store(g0, g1):
-            for g in range(g0, g1):
-                nc.sync.dma_start(out=out_rows[:, :, g * GROUP : (g + 1) * GROUP], in_=stage[:, g, :, :])
+        def store(u):
+            n0 = STARTS[u] * P
+            n1 = n0 + size(u) * P
+            nc.sync.dma_start(
+                out=out_rows[:, :, n0:n1], in_=stage[:, 2 * n0 : 2 * n1].rearrange("p (m n) -> p m n", m=2)
+            )
 
-        square_s(-1, 0)
-        square_v(-1, 1)
-        square_s(0, 0)
-        square_v(0, 2)
-        root(-1)
-        square_s(0, 1)
-        square_v(0, 3)
-        clamp(-1)
-
-        wps = ps_m.tile([P, GROUP], F32, name="acc")
+        zc = const.tile([P, B], U32, align_bytes=64)
+        zs = const.tile([P, B], U8, align_bytes=64)
+        wps = ps_m.tile([P, MAXJ * P], F32, name="acc")
         nc.tensor.matmul(out=wps[:, 0:4], lhsT=ones[:], rhs=wrow[:], start=True, stop=True)
+        done = [0]
+        unit_of = [u for u in range(UNITS) for j in range(SIZES[u])]
+
+        def square_next():
+            t = done[0]
+            u = unit_of[t]
+            square_s(u, t - STARTS[u])
+            if t == STARTS[u] and u > 2:
+                root(u - 1)
+            done[0] += 1
+            if done[0] == TILES:
+                root(u)
+
+        square_s(Z, 0)
+        square_v(Z, 1)
+        square_s(0, 0)
+        square_v(0, 1)
+        root(Z)
+        clamp(Z)
+        square_s(0, 3)
+        square_v(0, 2)
+        square_s(1, 0)
+        square_s(1, 1)
+        root(0)
+        normalise(Z)
+        transposes(Z)
         wf = const.tile([P, 3], F32)
         nc.vector.tensor_copy(out=wf[:], in_=wps[:, 0:3])
         wmax = const.tile([P, 1], F32)
@@ -212,43 +253,64 @@ def tile_multiscalecosinefusion_kernel(tc, z_ego, exo_bank, weights, out):
         scale = const.tile([P, 1], F32)
         nc.gpsimd.tensor_tensor(out=scale[:], in0=n012[:], in1=rsum[:], op=ALU.mult)
 
-        normalise(-1)
-        root(0)
+        square_v(1, 3)
         clamp(0)
-        transposes(-1)
-        new_grp(-1)
-        copy_out(-1, 0, "v")
+        square_v(1, 2)
         normalise(0)
         transposes(0)
-        for j in range(GJ):
-            square_s(1, j)
-        zc = const.tile([P, B], U32, align_bytes=64)
-        zs = const.tile([P, B], U8, align_bytes=64)
-        nc.vector.quantize_mx(out=zc[:].bitcast(FP8X4), scales=zs[:], in_=grp[-1][:, : 4 * B])
+        done[0] = STARTS[2]
+        square_next()
+        square_next()
+        root(1)
+        new_grp(Z)
+        copy_out(Z, 0, "v")
+        clamp(1)
+        new_grp(0)
+        copy_out(0, 0, "v")
+        while done[0] < STARTS[4] + 1:
+            square_next()
+        normalise(1)
+        transposes(1)
+        nc.vector.quantize_mx(out=zc[:].bitcast(FP8X4), scales=zs[:], in_=grp[Z][:, : 4 * B])
 
-        for g in range(GROUPS + 1):
-            if g == 0:
-                root(1)
-            late = g >= GROUPS - 2
-            if g + 2 < GROUPS:
-                for j in range(GJ):
-                    square_s(g + 2, j)
-            if g < GROUPS:
-                new_grp(g)
-                copy_out(g, 0, "v")
-            if g + 1 < GROUPS:
-                clamp(g + 1)
-            if g < GROUPS:
-                copy_out(g, 1, "s" if late else "v")
-            if g + 1 < GROUPS:
-                normalise(g + 1)
-                transposes(g + 1)
-            if g < GROUPS:
-                quantise(g)
-                multiply(g)
-            if g > 0:
-                result(g - 1, 0, "s" if late and g < GROUPS else "v")
-                result(g - 1, 1, "s")
-                store(g - 1, g)
-            if g + 2 < GROUPS:
-                root(g + 2)
+        for u in range(LAST):
+            late = u >= 12
+            while done[0] < min(TILES, STARTS[u] + 20 + 0):
+                square_next()
+            if late:
+                clamp(u + 2)
+            if u > 0:
+                if u not in grp:
+                    new_grp(u)
+                copy_out(u, 0, "v")
+            if not late:
+                clamp(u + 2)
+            if u <= 12:
+                copy_out(u, 1, "v")
+            normalise(u + 2)
+            transposes(u + 2)
+            quantise(u)
+            multiply(u)
+            if late and u + 1 < LAST:
+                new_grp(u + 1)
+                copy_out(u + 1, 1, "s")
+            if u > 0:
+                result(u - 1, 0, "s" if late else "v")
+                if u - 1 in (1,):
+                    result(u - 1, 1, "v")
+                elif u > 12:
+                    result(u - 1, 1, "s")
+                store(u - 1)
+            if not late and u not in (1,):
+                result(u, 1, "s")
+
+        for u in (LAST, LAST + 1):
+            new_grp(u)
+            copy_out(u, 0, "v" if u == LAST else "v")
+        for u in (LAST, LAST + 1):
+            quantise(u)
+            multiply(u)
+        for u in (LAST - 1, LAST, LAST + 1):
+            result(u, 0, "v")
+            result(u, 1, "s")
+            store(u)

@@ -69,6 +69,13 @@ def tile_multiscalecosinefusion_kernel(tc, z_ego, exo_bank, weights, out):
         nc.vector.memset(ones[:], 1.0)
         two = const.tile([P, 3], F32)
         nc.vector.memset(two[:], 2.0)
+        unit3 = const.tile([P, 3], F32)
+        nc.vector.memset(unit3[:], 1.0)
+        inv_temps = const.tile([P, 3], F32)
+        for i in range(3):
+            nc.gpsimd.tensor_scalar(
+                out=inv_temps[:, i : i + 1], in0=unit3[:, i : i + 1], scalar1=INV_TEMPS[i], scalar2=None, op0=ALU.mult
+            )
         minus1 = const.tile([P, 1], F32)
         nc.vector.memset(minus1[:], -1.0)
         warm = const.tile([P, 1], F32)
@@ -226,32 +233,13 @@ def tile_multiscalecosinefusion_kernel(tc, z_ego, exo_bank, weights, out):
         nc.vector.tensor_copy(out=wf[:], in_=wps[:, 0:3])
         wmax = const.tile([P, 1], F32)
         nc.vector.reduce_max(out=wmax[:], in_=wps[:, 0:3], axis=AX.X)
-
-        wd = const.tile([P, 3], F32)
-        nc.gpsimd.tensor_scalar(
-            out=wd[:], in0=wf[:], scalar1=wmax[:, 0:1], scalar2=None, op0=ALU.subtract
-        )
         wl = const.tile([P, 3], F32)
-        nc.gpsimd.tensor_scalar(out=wl[:], in0=wd[:], scalar1=LOG2E, scalar2=None, op0=ALU.mult)
-        ew = const.tile([P, 3], F32)
-        nc.gpsimd.tensor_tensor(out=ew[:], in0=two[:], in1=wl[:], op=ALU.pow)
-        terms = const.tile([P, 3], F32)
-        for i in range(3):
-            nc.gpsimd.tensor_scalar(
-                out=terms[:, i : i + 1], in0=ew[:, i : i + 1], scalar1=INV_TEMPS[i], scalar2=None, op0=ALU.mult
-            )
-        s01 = const.tile([P, 1], F32)
-        nc.gpsimd.tensor_tensor(out=s01[:], in0=ew[:, 0:1], in1=ew[:, 1:2], op=ALU.add)
-        s012 = const.tile([P, 1], F32)
-        nc.gpsimd.tensor_tensor(out=s012[:], in0=s01[:], in1=ew[:, 2:3], op=ALU.add)
-        n01 = const.tile([P, 1], F32)
-        nc.gpsimd.tensor_tensor(out=n01[:], in0=terms[:, 0:1], in1=terms[:, 1:2], op=ALU.add)
-        n012 = const.tile([P, 1], F32)
-        nc.gpsimd.tensor_tensor(out=n012[:], in0=n01[:], in1=terms[:, 2:3], op=ALU.add)
-        rsum = const.tile([P, 1], F32)
-        nc.gpsimd.tensor_tensor(out=rsum[:], in0=s012[:], in1=minus1[:], op=ALU.pow)
-        scale = const.tile([P, 1], F32)
-        nc.gpsimd.tensor_tensor(out=scale[:], in0=n012[:], in1=rsum[:], op=ALU.mult)
+        nc.gpsimd.tensor_scalar(
+            out=wl[:], in0=wf[:], scalar1=wmax[:, 0:1], scalar2=LOG2E, op0=ALU.subtract, op1=ALU.mult
+        )
+        both = const.tile([P, 2, 3], F32)
+        nc.gpsimd.tensor_tensor(out=both[:, 1, :], in0=two[:], in1=wl[:], op=ALU.pow)
+        nc.gpsimd.tensor_tensor(out=both[:, 0, :], in0=both[:, 1, :], in1=inv_temps[:], op=ALU.mult)
 
         square_v(1, 3)
         clamp(0)
@@ -265,6 +253,12 @@ def tile_multiscalecosinefusion_kernel(tc, z_ego, exo_bank, weights, out):
         new_grp(Z)
         copy_out(Z, 0, "v")
         clamp(1)
+        sums = const.tile([P, 2], F32)
+        nc.vector.reduce_sum(out=sums[:], in_=both[:], axis=AX.X)
+        rsum = const.tile([P, 1], F32)
+        nc.gpsimd.tensor_tensor(out=rsum[:], in0=sums[:, 1:2], in1=minus1[:], op=ALU.pow)
+        scale = const.tile([P, 1], F32)
+        nc.gpsimd.tensor_tensor(out=scale[:], in0=sums[:, 0:1], in1=rsum[:], op=ALU.mult)
         new_grp(0)
         copy_out(0, 0, "v")
         while done[0] < STARTS[4] + 1:

@@ -76,10 +76,8 @@ def tile_multiscalecosinefusion_kernel(tc, z_ego, exo_bank, weights, out):
             nc.gpsimd.tensor_scalar(
                 out=inv_temps[:, i : i + 1], in0=unit3[:, i : i + 1], scalar1=INV_TEMPS[i], scalar2=None, op0=ALU.mult
             )
-        minus1 = const.tile([P, 1], F32)
-        nc.vector.memset(minus1[:], -1.0)
         warm = const.tile([P, 1], F32)
-        nc.scalar.activation(out=warm[:], in_=minus1[:], func=ACT.Abs_reciprocal_sqrt)
+        nc.scalar.activation(out=warm[:], in_=unit3[:, 0:1], func=ACT.Abs_reciprocal_sqrt)
         ident = const.tile([P, P], F32)
         make_identity(nc, ident[:])
 
@@ -229,23 +227,20 @@ def tile_multiscalecosinefusion_kernel(tc, z_ego, exo_bank, weights, out):
         root(0)
         normalise(Z)
         transposes(Z)
-        wf = const.tile([P, 3], F32)
-        nc.vector.tensor_copy(out=wf[:], in_=wps[:, 0:3])
+        square_v(1, 3)
+        clamp(0)
+        square_v(1, 2)
         wmax = const.tile([P, 1], F32)
         nc.vector.reduce_max(out=wmax[:], in_=wps[:, 0:3], axis=AX.X)
+        normalise(0)
+        transposes(0)
         wl = const.tile([P, 3], F32)
-        nc.gpsimd.tensor_scalar(
-            out=wl[:], in0=wf[:], scalar1=wmax[:, 0:1], scalar2=LOG2E, op0=ALU.subtract, op1=ALU.mult
+        nc.vector.tensor_scalar(
+            out=wl[:], in0=wps[:, 0:3], scalar1=wmax[:, 0:1], scalar2=LOG2E, op0=ALU.subtract, op1=ALU.mult
         )
         both = const.tile([P, 2, 3], F32)
         nc.gpsimd.tensor_tensor(out=both[:, 1, :], in0=two[:], in1=wl[:], op=ALU.pow)
         nc.gpsimd.tensor_tensor(out=both[:, 0, :], in0=both[:, 1, :], in1=inv_temps[:], op=ALU.mult)
-
-        square_v(1, 3)
-        clamp(0)
-        square_v(1, 2)
-        normalise(0)
-        transposes(0)
         done[0] = STARTS[2]
         square_next()
         square_next()
@@ -253,33 +248,35 @@ def tile_multiscalecosinefusion_kernel(tc, z_ego, exo_bank, weights, out):
         new_grp(Z)
         copy_out(Z, 0, "v")
         clamp(1)
-        sums = const.tile([P, 2], F32)
-        nc.vector.reduce_sum(out=sums[:], in_=both[:], axis=AX.X)
-        rsum = const.tile([P, 1], F32)
-        nc.gpsimd.tensor_tensor(out=rsum[:], in0=sums[:, 1:2], in1=minus1[:], op=ALU.pow)
-        scale = const.tile([P, 1], F32)
-        nc.gpsimd.tensor_tensor(out=scale[:], in0=sums[:, 0:1], in1=rsum[:], op=ALU.mult)
         new_grp(0)
         copy_out(0, 0, "v")
         while done[0] < STARTS[4] + 1:
             square_next()
         normalise(1)
         transposes(1)
+        sums = const.tile([P, 2], F32)
+        nc.vector.reduce_sum(out=sums[:], in_=both[:], axis=AX.X)
         nc.vector.quantize_mx(out=zc[:].bitcast(FP8X4), scales=zs[:], in_=grp[Z][:, : 4 * B])
+        rsum = const.tile([P, 1], F32)
+        nc.vector.reciprocal(rsum[:], sums[:, 1:2])
+        clamp(2)
+        copy_out(0, 1, "v")
+        scale = const.tile([P, 1], F32)
+        nc.vector.tensor_tensor(out=scale[:], in0=sums[:, 0:1], in1=rsum[:], op=ALU.mult)
 
         for u in range(LAST):
             late = u >= 12
-            while done[0] < min(TILES, STARTS[u] + 20 + 0):
+            while done[0] < min(TILES, STARTS[u] + 21):
                 square_next()
-            if late:
+            if u > 12:
                 clamp(u + 2)
             if u > 0:
                 if u not in grp:
                     new_grp(u)
                 copy_out(u, 0, "v")
-            if not late:
+            if 0 < u <= 12:
                 clamp(u + 2)
-            if u <= 12:
+            if 0 < u <= 12:
                 copy_out(u, 1, "v")
             normalise(u + 2)
             transposes(u + 2)

@@ -254,15 +254,12 @@ def tile_multiscalecosinefusion_kernel(tc, z_ego, exo_bank, weights, out):
             square_next()
         normalise(1)
         transposes(1)
-        sums = const.tile([P, 2], F32)
-        nc.vector.reduce_sum(out=sums[:], in_=both[:], axis=AX.X)
         nc.vector.quantize_mx(out=zc[:].bitcast(FP8X4), scales=zs[:], in_=grp[Z][:, : 4 * B])
-        rsum = const.tile([P, 1], F32)
-        nc.vector.reciprocal(rsum[:], sums[:, 1:2])
         clamp(2)
         copy_out(0, 1, "v")
+        sums = const.tile([P, 2], F32)
+        rsum = const.tile([P, 1], F32)
         scale = const.tile([P, 1], F32)
-        nc.vector.tensor_tensor(out=scale[:], in0=sums[:, 0:1], in1=rsum[:], op=ALU.mult)
 
         for u in range(LAST):
             late = u >= 12
@@ -273,11 +270,17 @@ def tile_multiscalecosinefusion_kernel(tc, z_ego, exo_bank, weights, out):
             if u > 0:
                 if u not in grp:
                     new_grp(u)
+                if u == 1:
+                    nc.vector.reduce_sum(out=sums[:], in_=both[:], axis=AX.X)
                 copy_out(u, 0, "v")
+                if u == 1:
+                    nc.vector.reciprocal(rsum[:], sums[:, 1:2])
             if 0 < u <= 12:
                 clamp(u + 2)
             if 0 < u <= 12:
                 copy_out(u, 1, "v")
+                if u == 1:
+                    nc.vector.tensor_tensor(out=scale[:], in0=sums[:, 0:1], in1=rsum[:], op=ALU.mult)
             normalise(u + 2)
             transposes(u + 2)
             quantise(u)
@@ -285,6 +288,8 @@ def tile_multiscalecosinefusion_kernel(tc, z_ego, exo_bank, weights, out):
             if late and u + 1 < LAST:
                 new_grp(u + 1)
                 copy_out(u + 1, 1, "s")
+            if u == 1:
+                result(0, 1, "s")
             if u > 0:
                 result(u - 1, 0, "s" if late else "v")
                 if u - 1 in (1,):
@@ -292,7 +297,7 @@ def tile_multiscalecosinefusion_kernel(tc, z_ego, exo_bank, weights, out):
                 elif u > 12:
                     result(u - 1, 1, "s")
                 store(u - 1)
-            if not late and u not in (1,):
+            if not late and u not in (0, 1):
                 result(u, 1, "s")
 
         for u in (LAST, LAST + 1):

@@ -263,7 +263,7 @@ def tile_multiscalecosinefusion_kernel(tc, z_ego, exo_bank, weights, out):
 
         for u in range(LAST):
             late = u >= 12
-            while done[0] < min(TILES, STARTS[u] + 21):
+            while done[0] < min(TILES, STARTS[u] + 22):
                 square_next()
             if u > 12:
                 clamp(u + 2)
@@ -302,11 +302,15 @@ def tile_multiscalecosinefusion_kernel(tc, z_ego, exo_bank, weights, out):
 
         for u in (LAST, LAST + 1):
             new_grp(u)
-            copy_out(u, 0, "v" if u == LAST else "v")
+            copy_out(u, 0, "v")
+        quantise(LAST)
+        multiply(LAST)
+        result(LAST - 1, 0, "v")
+        result(LAST - 1, 1, "s")
+        store(LAST - 1)
+        quantise(LAST + 1)
+        multiply(LAST + 1)
         for u in (LAST, LAST + 1):
-            quantise(u)
-            multiply(u)
-        for u in (LAST - 1, LAST, LAST + 1):
             result(u, 0, "v")
             result(u, 1, "s")
             store(u)

@@ -123,13 +123,28 @@ def tile_multiscalecosinefusion_kernel(tc, z_ego, exo_bank, weights, out):
         acc = {}
 
         def normalise(u):
-            t = xnp.tile([P, MAXJ, D], BF16, name="xn")
-            xn[u] = t
+            if u not in xn:
+                t = xnp.tile([P, MAXJ, D], BF16, name="xn")
+                xn[u] = t
+            t = xn[u]
             for j in range(size(u)):
                 c = col(u) + j
+                if u > 2 and j in (3,):
+                    continue
                 nc.vector.tensor_scalar(
                     out=t[:, j, :], in0=raw(u, j), scalar1=rinv[:, c : c + 1], scalar2=None, op0=ALU.mult
                 )
+
+        def normalise_g(u):
+            t = xnp.tile([P, MAXJ, D], BF16, name="xn")
+            xn[u] = t
+            for j in (3,):
+                c = col(u) + j
+                if u > 2 and j < size(u):
+                    nc.gpsimd.tensor_scalar(
+                        out=t[:, j, :], in0=raw(u, j), scalar1=rinv[:, c : c + 1], scalar2=1.0,
+                        op0=ALU.mult, op1=ALU.mult,
+                    )
 
         def transposes(u):
             for h in range(size(u) // 2):
@@ -262,11 +277,8 @@ def tile_multiscalecosinefusion_kernel(tc, z_ego, exo_bank, weights, out):
         scale = const.tile([P, 1], F32)
 
         for u in range(LAST):
-            late = u >= 12
             while done[0] < min(TILES, STARTS[u] + 22):
                 square_next()
-            if u > 12:
-                clamp(u + 2)
             if u > 0:
                 if u not in grp:
                     new_grp(u)
@@ -276,28 +288,30 @@ def tile_multiscalecosinefusion_kernel(tc, z_ego, exo_bank, weights, out):
                 if u == 1:
                     nc.vector.reciprocal(rsum[:], sums[:, 1:2])
             if 0 < u <= 12:
-                clamp(u + 2)
-            if 0 < u <= 12:
                 copy_out(u, 1, "v")
                 if u == 1:
                     nc.vector.tensor_tensor(out=scale[:], in0=sums[:, 0:1], in1=rsum[:], op=ALU.mult)
             normalise(u + 2)
             transposes(u + 2)
             quantise(u)
+            if u + 3 < UNITS:
+                clamp(u + 3)
+                normalise_g(u + 3)
             multiply(u)
-            if late and u + 1 < LAST:
+            if u >= 12 and u + 1 < LAST:
                 new_grp(u + 1)
                 copy_out(u + 1, 1, "s")
             if u == 1:
                 result(0, 1, "s")
             if u > 0:
-                result(u - 1, 0, "s" if late else "v")
-                if u - 1 in (1,):
+                if u == 1 or u >= 0:
+                    result(u - 1, 0, "s" if u >= 12 else "v")
+                if u - 1 in (1, 5):
                     result(u - 1, 1, "v")
                 elif u > 12:
                     result(u - 1, 1, "s")
                 store(u - 1)
-            if not late and u not in (0, 1):
+            if 0 < u < 12 and u not in (1, 5):
                 result(u, 1, "s")
 
         for u in (LAST, LAST + 1):

from contextlib import ExitStack

import concourse.mybir as mybir
from concourse.masks import make_identity

FLOPS = 2 * 256 * 8192 * 512

F32 = mybir.dt.float32
BF16 = mybir.dt.bfloat16
U32 = mybir.dt.uint32
U8 = mybir.dt.uint8
FP8X4 = mybir.dt.float8_e4m3fn_x4
ACT = mybir.ActivationFunctionType
ALU = mybir.AluOpType
AX = mybir.AxisListType

P = 128
D = 512
B = 256
N = 8192
TILES = N // P
ZJ = B // P
SIZES = [4] * 15 + [2, 2]
STARTS = [sum(SIZES[:u]) for u in range(len(SIZES))]
UNITS = len(SIZES)
MAXJ = max(SIZES)
LAST = UNITS - 2
Z = -1
INV_TEMPS = (1.0 / 0.07, 1.0 / 0.1, 1.0 / 0.2)
LOG2E = 1.4426950408889634
MAX_RINV = 1e8


def tile_multiscalecosinefusion_kernel(tc, z_ego, exo_bank, weights, out):
    nc = tc.nc
    with ExitStack() as ctx:
        const = ctx.enter_context(tc.tile_pool(name="const", bufs=1))
        junkp = ctx.enter_context(tc.tile_pool(name="junkp", bufs=2))
        xnp = ctx.enter_context(tc.tile_pool(name="xnp", bufs=4))
        grpp = ctx.enter_context(tc.tile_pool(name="grpp", bufs=3))
        qp = ctx.enter_context(tc.tile_pool(name="qp", bufs=3))
        ps_t = ctx.enter_context(tc.psum_pool(name="ps_t", bufs=4))
        ps_m = ctx.enter_context(tc.psum_pool(name="ps_m", bufs=4))
        ctx.enter_context(tc.manual_schedule())

        zraw = const.tile([P, ZJ, D], BF16)
        xraw = const.tile([P, TILES, D], BF16)
        wrow = const.tile([P, 4], BF16)
        nc.vector.memset(wrow[:], 0.0)

        def rows_of(u):
            return exo_bank[STARTS[u] * P : (STARTS[u] + SIZES[u]) * P, :].rearrange("(p j) d -> p j d", p=P)

        def load(u, j0, j1):
            nc.sync.dma_start(out=xraw[:, STARTS[u] + j0 : STARTS[u] + j1, :], in_=rows_of(u)[:, j0:j1, :])

        z_rows = z_ego.rearrange("(p j) d -> p j d", j=ZJ)
        for j in range(ZJ):
            nc.sync.dma_start(out=zraw[:, j, :], in_=z_rows[:, j, :])
        for u in range(3):
            load(u, 0, 2)
            load(u, 2, 4)
            if u == 0:
                nc.sync.dma_start(out=wrow[0:1, 0:3], in_=weights.unsqueeze(0))
        for u in range(3, UNITS):
            load(u, 0, SIZES[u])

        ones = const.tile([P, P], BF16)
        nc.vector.memset(ones[:], 1.0)
        two = const.tile([P, 3], F32)
        nc.vector.memset(two[:], 2.0)
        unit3 = const.tile([P, 3], F32)
        nc.vector.memset(unit3[:], 1.0)
        inv_temps = const.tile([P, 3], F32)
        for i in range(3):
            nc.gpsimd.tensor_scalar(
                out=inv_temps[:, i : i + 1], in0=unit3[:, i : i + 1], scalar1=INV_TEMPS[i], scalar2=None, op0=ALU.mult
            )
        warm = const.tile([P, 1], F32)
        nc.scalar.activation(out=warm[:], in_=unit3[:, 0:1], func=ACT.Abs_reciprocal_sqrt)
        ident = const.tile([P, P], F32)
        make_identity(nc, ident[:])

        ssp = const.tile([P, ZJ + TILES], F32)
        rsq = const.tile([P, ZJ + TILES], F32)
        rinv = const.tile([P, ZJ + TILES], F32)
        stage = const.tile([P, 2 * N], F32)

        def size(u):
            return ZJ if u == Z else SIZES[u]

        def col(u):
            return 0 if u == Z else ZJ + STARTS[u]

        def raw(u, j):
            return zraw[:, j, :] if u == Z else xraw[:, STARTS[u] + j, :]

        def square_s(u, j):
            junk = junkp.tile([P, D], BF16, name="junk_s")
            c = col(u) + j
            nc.scalar.activation(out=junk[:], in_=raw(u, j), func=ACT.Square, accum_out=ssp[:, c : c + 1])

        def square_v(u, j):
            junk = junkp.tile([P, D], BF16, name="junk_v")
            c = col(u) + j
            nc.vector.scalar_tensor_tensor(
                out=junk[:], in0=raw(u, j), scalar=1.0, in1=raw(u, j), op0=ALU.mult, op1=ALU.mult,
                accum_out=ssp[:, c : c + 1],
            )

        def root(u):
            c = slice(col(u), col(u) + size(u))
            nc.scalar.activation(out=rsq[:, c], in_=ssp[:, c], func=ACT.Abs_reciprocal_sqrt)

        def clamp(u):
            c = slice(col(u), col(u) + size(u))
            nc.vector.tensor_scalar(out=rinv[:, c], in0=rsq[:, c], scalar1=MAX_RINV, scalar2=None, op0=ALU.min)

        xn = {}
        pt = {}
        grp = {}
        codes = {}
        acc = {}

        def normalise(u):
            if u not in xn:
                t = xnp.tile([P, MAXJ, D], BF16, name="xn")
                xn[u] = t
            t = xn[u]
            for j in range(size(u)):
                c = col(u) + j
                if u > 2 and j in (3,):
                    continue
                nc.vector.tensor_scalar(
                    out=t[:, j, :], in0=raw(u, j), scalar1=rinv[:, c : c + 1], scalar2=None, op0=ALU.mult
                )

        def normalise_g(u):
            t = xnp.tile([P, MAXJ, D], BF16, name="xn")
            xn[u] = t
            for j in (3,):
                c = col(u) + j
                if u > 2 and j < size(u):
                    nc.gpsimd.tensor_scalar(
                        out=t[:, j, :], in0=raw(u, j), scalar1=rinv[:, c : c + 1], scalar2=1.0,
                        op0=ALU.mult, op1=ALU.mult,
                    )

        def transposes(u):
            for h in range(size(u) // 2):
                t = ps_t.tile([P, 2, 2, P], F32, name="pt")
                pt[u, h] = t
                for j in range(2):
                    words = xn[u][:, 2 * h + j, :].bitcast(F32)
                    for w in range(2):
                        nc.tensor.transpose(t[:, j, w, :], words[:, w * P : (w + 1) * P], ident[:])

        def new_grp(u):
            t = grpp.tile([P, MAXJ * P * 4], BF16, name="grp", align_bytes=64)
            grp[u] = t

        def copy_out(u, h, engine):
            dst = grp[u][:, h * 1024 : (h + 1) * 1024].bitcast(F32).rearrange("p (j r w) -> p j r w", j=2, w=2)
            src = pt[u, h][:].rearrange("p j w r -> p j r w")
            if engine == "v":
                nc.vector.tensor_copy(out=dst, in_=src)
            else:
                nc.scalar.copy(out=dst, in_=src)

        def quantise(u):
            n = size(u) * P
            c = qp.tile([P, MAXJ * P], U32, name="codes", align_bytes=64)
            s = qp.tile([P, MAXJ * P], U8, name="scl", align_bytes=64)
            codes[u] = (c, s)
            nc.vector.quantize_mx(out=c[:, :n].bitcast(FP8X4), scales=s[:, :n], in_=grp[u][:, : 4 * n])

        def multiply(u):
            n = size(u) * P
            for m in range(2):
                if size(u) < MAXJ:
                    a = ps_t.tile([P, 2, 2, P], F32, name="pt")
                    a = a[:].rearrange("p j w r -> p (j w r)")
                else:
                    a = ps_m.tile([P, MAXJ * P], F32, name="acc")
                acc[u, m] = a
                nc.tensor.matmul_mx(
                    out=a[:, :n],
                    lhsT=zc[:, m * P : (m + 1) * P].bitcast(FP8X4),
                    lhsT_scale=zs[:, m * P : (m + 1) * P],
                    rhs=codes[u][0][:, :n].bitcast(FP8X4),
                    rhs_scale=codes[u][1][:, :n],
                    start=True,
                    stop=True,
                )

        def result(u, m, engine):
            n = size(u) * P
            n0 = 2 * STARTS[u] * P + m * n
            dst = stage[:, n0 : n0 + n].rearrange("p (r j) -> p r j", j=size(u))
            src = acc[u, m][:, :n].rearrange("p (j r) -> p r j", j=size(u))
            if engine == "v":
                nc.vector.tensor_scalar(out=dst, in0=src, scalar1=scale[:, 0:1], scalar2=None, op0=ALU.mult)
            else:
                nc.scalar.activation(out=dst, in_=src, func=ACT.Copy, scale=scale[:, 0:1])

        out_rows = out.rearrange("(p m) n -> p m n", m=2)

        def store(u):
            n0 = STARTS[u] * P
            n1 = n0 + size(u) * P
            nc.sync.dma_start(
                out=out_rows[:, :, n0:n1], in_=stage[:, 2 * n0 : 2 * n1].rearrange("p (m n) -> p m n", m=2)
            )

        zc = const.tile([P, B], U32, align_bytes=64)
        zs = const.tile([P, B], U8, align_bytes=64)
        wps = ps_m.tile([P, MAXJ * P], F32, name="acc")
        nc.tensor.matmul(out=wps[:, 0:4], lhsT=ones[:], rhs=wrow[:], start=True, stop=True)
        done = [0]
        unit_of = [u for u in range(UNITS) for j in range(SIZES[u])]

        def square_next():
            t = done[0]
            u = unit_of[t]
            square_s(u, t - STARTS[u])
            if t == STARTS[u] and u > 2:
                root(u - 1)
            done[0] += 1
            if done[0] == TILES:
                root(u)

        square_s(Z, 0)
        square_v(Z, 1)
        square_s(0, 0)
        square_v(0, 1)
        root(Z)
        clamp(Z)
        square_s(0, 3)
        square_v(0, 2)
        square_s(1, 0)
        square_s(1, 1)
        root(0)
        normalise(Z)
        transposes(Z)
        square_v(1, 3)
        clamp(0)
        square_v(1, 2)
        wmax = const.tile([P, 1], F32)
        nc.vector.reduce_max(out=wmax[:], in_=wps[:, 0:3], axis=AX.X)
        normalise(0)
        transposes(0)
        wl = const.tile([P, 3], F32)
        nc.vector.tensor_scalar(
            out=wl[:], in0=wps[:, 0:3], scalar1=wmax[:, 0:1], scalar2=LOG2E, op0=ALU.subtract, op1=ALU.mult
        )
        both = const.tile([P, 2, 3], F32)
        nc.gpsimd.tensor_tensor(out=both[:, 1, :], in0=two[:], in1=wl[:], op=ALU.pow)
        nc.gpsimd.tensor_tensor(out=both[:, 0, :], in0=both[:, 1, :], in1=inv_temps[:], op=ALU.mult)
        done[0] = STARTS[2]
        square_next()
        square_next()
        root(1)
        new_grp(Z)
        copy_out(Z, 0, "v")
        clamp(1)
        new_grp(0)
        copy_out(0, 0, "v")
        while done[0] < STARTS[4] + 1:
            square_next()
        normalise(1)
        transposes(1)
        nc.vector.quantize_mx(out=zc[:].bitcast(FP8X4), scales=zs[:], in_=grp[Z][:, : 4 * B])
        clamp(2)
        copy_out(0, 1, "v")
        sums = const.tile([P, 2], F32)
        rsum = const.tile([P, 1], F32)
        scale = const.tile([P, 1], F32)

        for u in range(LAST):
            while done[0] < min(TILES, STARTS[u] + 22):
                square_next()
            if u > 0:
                if u not in grp:
                    new_grp(u)
                if u == 1:
                    nc.vector.reduce_sum(out=sums[:], in_=both[:], axis=AX.X)
                copy_out(u, 0, "v")
                if u == 1:
                    nc.vector.reciprocal(rsum[:], sums[:, 1:2])
            if 0 < u <= 12:
                copy_out(u, 1, "v")
                if u == 1:
                    nc.vector.tensor_tensor(out=scale[:], in0=sums[:, 0:1], in1=rsum[:], op=ALU.mult)
            normalise(u + 2)
            transposes(u + 2)
            quantise(u)
            if u + 3 < UNITS:
                clamp(u + 3)
                normalise_g(u + 3)
            multiply(u)
            if u >= 12 and u + 1 < LAST:
                new_grp(u + 1)
                copy_out(u + 1, 1, "s")
            if u == 1:
                result(0, 1, "s")
            if u > 0:
                if u == 1 or u >= 0:
                    result(u - 1, 0, "s" if u >= 12 else "v")
                if u - 1 in (1, 5):
                    result(u - 1, 1, "v")
                elif u > 12:
                    result(u - 1, 1, "s")
                store(u - 1)
            if 0 < u < 12 and u not in (1, 5):
                result(u, 1, "s")

        for u in (LAST, LAST + 1):
            new_grp(u)
            copy_out(u, 0, "v")
        quantise(LAST)
        multiply(LAST)
        result(LAST - 1, 0, "v")
        result(LAST - 1, 1, "s")
        store(LAST - 1)
        quantise(LAST + 1)
        multiply(LAST + 1)
        for u in (LAST, LAST + 1):
            result(u, 0, "v")
            result(u, 1, "s")
            store(u)
